import numpy as np
import ml_dtypes


def mxq(x, axis, fmt="e4m3"):
    dtype, down = {"e4m3": (ml_dtypes.float8_e4m3fn, 7), "e5m2": (ml_dtypes.float8_e5m2, 14)}[fmt]
    v = np.moveaxis(np.asarray(x, np.float32).astype(ml_dtypes.bfloat16).astype(np.float64), axis, -1)
    blocks = v.reshape(v.shape[:-1] + (-1, 32))
    amax = np.abs(blocks).max(-1, keepdims=True)
    byte = np.maximum(np.where(amax > 0, np.frexp(amax)[1] - 1 + 127, 0) - down, 1)
    scale = np.exp2(byte - 127.0)
    codes = (blocks / scale).astype(np.float32).astype(dtype).astype(np.float64)
    return np.moveaxis((codes * scale).reshape(v.shape), -1, axis)


WIDE = False


def mx_kscale(k):
    if not WIDE:
        return np.ones(k)
    levels = np.array([20, -20, 10, -10, 0])
    a = np.random.permutation(np.resize(levels, k // 512 * 4)).reshape(k // 512, 4)
    idx = np.arange(k)
    return np.exp2(a[idx // 512, idx % 128 // 32])


BF16 = ml_dtypes.bfloat16


def bf(x):
    return np.asarray(x, np.float32).astype(BF16)


def f64(x):
    return np.asarray(x).astype(np.float64)


B, Nb1, Nw1, Nb2x, Nb2y, Nw2x, Nw2y, R, C = 4096, 2, 16, 1, 1, 32, 16, 128, 2
J1 = Nb1 * Nb1
J3 = Nb2x * Nb2y
J2 = J3 * J1
K3 = J1 * R
L3 = C * Nw2x * Nw2y


def to_grid(y):
    y = y.reshape(B, Nb2x, Nb2y, Nw2x, Nw2y, C).transpose(0, 1, 3, 2, 4, 5)
    return y.reshape(B, Nb2x * Nw2x, Nb2y * Nw2y, C)


def from_grid(g):
    g = g.reshape(B, Nb2x, Nw2x, Nb2y, Nw2y, C).transpose(0, 1, 3, 2, 4, 5)
    return g.reshape(B, J3, L3)


def setup_inputs():
    u = mx_kscale(L3)
    h_switch = np.random.standard_normal((B, J2, R))
    k2 = np.random.standard_normal((J2, R, R)) / np.sqrt(R)
    b2 = np.random.standard_normal((1, J2, R)) * 0.3
    k3 = np.random.standard_normal((J3, K3, L3)) / np.sqrt(K3) / u[None, None, :]
    b3 = np.random.standard_normal((1, J3, L3)) * 0.3
    g = np.random.standard_normal((B, J3, L3)) * np.exp2(np.random.randint(-12, 1, (B, 1, 1))) * 4.0 * u[None, None, :]
    return {"h_switch": bf(h_switch), "k2": bf(k2), "b2": bf(b2), "k3": bf(k3), "b3": bf(b3),
            "grad_out": bf(to_grid(g))}


def reference(h_switch, k2, b2, k3, b3, grad_out):
    dy = from_grid(f64(grad_out))
    dyq = mxq(dy, 2, "e5m2").transpose(1, 0, 2)
    k3q = mxq(f64(k3), 2, "e4m3").transpose(0, 2, 1)
    dg = (dyq @ k3q).transpose(1, 0, 2)
    dg = dg.reshape(B, J2, R)
    dh = dg.transpose(1, 0, 2) @ f64(k2).transpose(0, 2, 1)
    return dh.transpose(1, 0, 2)

@@ -1,0 +1,156 @@
+from contextlib import ExitStack
+
+import concourse.mybir as mybir
+from concourse.masks import make_identity
+
+F32 = mybir.dt.float32
+BF16 = mybir.dt.bfloat16
+U32 = mybir.dt.uint32
+U8 = mybir.dt.uint8
+E4M3X4 = mybir.dt.float8_e4m3fn_x4
+E5M2X4 = mybir.dt.float8_e5m2_x4
+
+P = 128
+SAMPLES = 4096
+WINDOW = 1024
+GROUPS = 4
+R = 128
+COEFFS = GROUPS * R
+
+K_PASS = 4 * P
+PASSES = WINDOW // K_PASS
+HALVES = 2
+BLOCK = 512
+TILES = BLOCK // P
+BLOCKS = SAMPLES // BLOCK
+ROWS_PER_PARTITION = SAMPLES // P
+
+FLOPS = 2 * SAMPLES * COEFFS * WINDOW + 2 * SAMPLES * COEFFS * R
+BYTES = 2 * SAMPLES * WINDOW + 2 * COEFFS * WINDOW + 2 * GROUPS * R * R + 4 * SAMPLES * COEFFS
+
+
+def quantise_row_tile(nc, pools, copy_out, ident, raw, fp8x4, codes, scales):
+    words = raw[:].bitcast(F32)
+    flipped = pools["flipped"].tile([P, PASSES, HALVES, P], F32, name="flipped")
+    for g in range(PASSES):
+        for u in range(HALVES):
+            first = (g * HALVES + u) * P
+            nc.tensor.transpose(flipped[:, g, u, :], words[:, first : first + P], ident[:])
+    grouped = pools["grouped"].tile([P, PASSES, P, HALVES], F32, name="grouped", align_bytes=64)
+    copy_out(out=grouped[:], in_=flipped[:].rearrange("p g u r -> p g r u"))
+    for g in range(PASSES):
+        nc.vector.quantize_mx(
+            out=codes[:, g, :].bitcast(fp8x4),
+            scales=scales[:, g, :],
+            in_=grouped[:, g, :, :].rearrange("p r u -> p (r u)").bitcast(BF16),
+        )
+
+
+def tile_switchnet_fstar_pb_t_kernel(tc, h_switch, k2, b2, k3, b3, grad_out, out):
+    nc = tc.nc
+
+    dy_rows = grad_out.rearrange("(p s) x y c -> p s (x y c)", s=ROWS_PER_PARTITION)
+    out_rows = out.rearrange("(p s) j i -> p s (j i)", s=ROWS_PER_PARTITION)
+    k3_rows = k3[0, :, :].rearrange("(j p) k -> p j k", p=P)
+
+    with ExitStack() as ctx:
+        ctx.enter_context(tc.manual_schedule())
+        keep = ctx.enter_context(tc.tile_pool(name="keep", bufs=1))
+        raw_pool = ctx.enter_context(tc.tile_pool(name="raw", bufs=GROUPS + BLOCKS * TILES))
+        pools = {
+            "grouped": ctx.enter_context(tc.tile_pool(name="grouped", bufs=4)),
+            "flipped": ctx.enter_context(tc.psum_pool(name="flipped", bufs=3)),
+        }
+        operand_pool = ctx.enter_context(tc.tile_pool(name="operand", bufs=2))
+        dg_pool = ctx.enter_context(tc.tile_pool(name="dg", bufs=2))
+        result_pool = ctx.enter_context(tc.tile_pool(name="result", bufs=8))
+        dg_psum = ctx.enter_context(tc.psum_pool(name="dg_psum", bufs=3))
+        product_psum = ctx.enter_context(tc.psum_pool(name="product_psum", bufs=2))
+
+        def bank_copy(index):
+            return nc.vector.tensor_copy if index % 2 == 0 else nc.scalar.copy
+
+        ident = keep.tile([P, P], F32)
+        make_identity(nc, ident[:])
+
+        k3_raw = []
+        for j in range(GROUPS):
+            raw = raw_pool.tile([P, WINDOW], BF16)
+            nc.sync.dma_start(out=raw[:], in_=k3_rows[:, j, :])
+            k3_raw.append(raw)
+        k2_rows = keep.tile([P, GROUPS, R], BF16)
+        dy_raw = []
+        for s in range(ROWS_PER_PARTITION):
+            raw = raw_pool.tile([P, WINDOW], BF16)
+            nc.sync.dma_start(out=raw[:], in_=dy_rows[:, s, :])
+            dy_raw.append(raw)
+            if s == TILES - 1:
+                nc.sync.dma_start(out=k2_rows[:], in_=k2.rearrange("j i o -> i j o"))
+
+        k3_codes = keep.tile([P, PASSES, COEFFS], U32, align_bytes=64)
+        k3_scales = keep.tile([P, PASSES, COEFFS], U8, align_bytes=64)
+        for j in range(GROUPS):
+            cols = slice(j * R, (j + 1) * R)
+            quantise_row_tile(
+                nc, pools, bank_copy(j), ident, k3_raw[j], E4M3X4, k3_codes[:, :, cols], k3_scales[:, :, cols]
+            )
+
+        def quantise_block(b):
+            dy_codes = operand_pool.tile([P, PASSES, BLOCK], U32, align_bytes=64)
+            dy_scales = operand_pool.tile([P, PASSES, BLOCK], U8, align_bytes=64)
+            for t in range(TILES):
+                cols = slice(t * P, (t + 1) * P)
+                quantise_row_tile(
+                    nc, pools, bank_copy(t), ident, dy_raw[b * TILES + t], E5M2X4,
+                    dy_codes[:, :, cols], dy_scales[:, :, cols],
+                )
+            return dy_codes, dy_scales
+
+        def mx_matmul(dy_codes, dy_scales):
+            dgT = dg_pool.tile([P, GROUPS, BLOCK], F32)
+            for j in range(GROUPS):
+                cols = slice(j * R, (j + 1) * R)
+                acc = dg_psum.tile([P, BLOCK], F32)
+                for g in range(PASSES):
+                    nc.tensor.matmul_mx(
+                        out=acc[:],
+                        lhsT=k3_codes[:, g, cols].bitcast(E4M3X4),
+                        lhsT_scale=k3_scales[:, g, cols],
+                        rhs=dy_codes[:, g, :].bitcast(E5M2X4),
+                        rhs_scale=dy_scales[:, g, :],
+                        start=(g == 0),
+                        stop=(g == PASSES - 1),
+                    )
+                bank_copy(j)(out=dgT[:, j, :], in_=acc[:])
+            return dgT
+
+        def second_matmul(b, dgT):
+            for t in range(TILES):
+                product = product_psum.tile([P, COEFFS], F32)
+                for j in range(GROUPS):
+                    nc.tensor.matmul(
+                        out=product[:, j * R : (j + 1) * R],
+                        lhsT=dgT[:, j, t * P : (t + 1) * P],
+                        rhs=k2T[:, j, :],
+                        start=True,
+                        stop=True,
+                    )
+                result = result_pool.tile([P, COEFFS], F32)
+                nc.scalar.copy(out=result[:], in_=product[:])
+                nc.sync.dma_start(out=out_rows[:, b * TILES + t, :], in_=result[:])
+
+        operands = quantise_block(0)
+
+        k2_f32 = keep.tile([P, GROUPS, R], F32)
+        nc.vector.tensor_copy(out=k2_f32[:], in_=k2_rows[:])
+        k2T_psum = pools["flipped"].tile([P, GROUPS, R], F32, tag="flipped")
+        for j in range(GROUPS):
+            nc.tensor.transpose(k2T_psum[:, j, :], k2_f32[:, j, :], ident[:])
+        k2T = keep.tile([P, GROUPS, R], F32)
+        nc.vector.tensor_copy(out=k2T[:], in_=k2T_psum[:])
+
+        for b in range(BLOCKS):
+            dgT = mx_matmul(*operands)
+            if b + 1 < BLOCKS:
+                operands = quantise_block(b + 1)
+            second_matmul(b, dgT)

@@ -24,20 +24,21 @@ BLOCK = 512
 TILES = BLOCK // P
 BLOCKS = SAMPLES // BLOCK
 ROWS_PER_PARTITION = SAMPLES // P
+PSUM_BANKS = 8
 
 FLOPS = 2 * SAMPLES * COEFFS * WINDOW + 2 * SAMPLES * COEFFS * R
 BYTES = 2 * SAMPLES * WINDOW + 2 * COEFFS * WINDOW + 2 * GROUPS * R * R + 4 * SAMPLES * COEFFS
 
 
-def quantise_row_tile(nc, pools, copy_out, ident, raw, fp8x4, codes, scales):
+def quantise_row_tile(nc, banks, grouped_pool, ident, raw, fp8x4, codes, scales):
     words = raw[:].bitcast(F32)
-    flipped = pools["flipped"].tile([P, PASSES, HALVES, P], F32, name="flipped")
+    flipped = banks.tile([P, PASSES, HALVES, P], F32, tag="bank")
     for g in range(PASSES):
         for u in range(HALVES):
             first = (g * HALVES + u) * P
             nc.tensor.transpose(flipped[:, g, u, :], words[:, first : first + P], ident[:])
-    grouped = pools["grouped"].tile([P, PASSES, P, HALVES], F32, name="grouped", align_bytes=64)
-    copy_out(out=grouped[:], in_=flipped[:].rearrange("p g u r -> p g r u"))
+    grouped = grouped_pool.tile([P, PASSES, P, HALVES], F32, align_bytes=64)
+    nc.scalar.copy(out=grouped[:], in_=flipped[:].rearrange("p g u r -> p g r u"))
     for g in range(PASSES):
         nc.vector.quantize_mx(
             out=codes[:, g, :].bitcast(fp8x4),
@@ -57,43 +58,27 @@ def tile_switchnet_fstar_pb_t_kernel(tc, h_switch, k2, b2, k3, b3, grad_out, out
         ctx.enter_context(tc.manual_schedule())
         keep = ctx.enter_context(tc.tile_pool(name="keep", bufs=1))
         raw_pool = ctx.enter_context(tc.tile_pool(name="raw", bufs=GROUPS + BLOCKS * TILES))
-        pools = {
-            "grouped": ctx.enter_context(tc.tile_pool(name="grouped", bufs=4)),
-            "flipped": ctx.enter_context(tc.psum_pool(name="flipped", bufs=3)),
-        }
+        grouped_pool = ctx.enter_context(tc.tile_pool(name="grouped", bufs=4))
         operand_pool = ctx.enter_context(tc.tile_pool(name="operand", bufs=2))
         dg_pool = ctx.enter_context(tc.tile_pool(name="dg", bufs=2))
-        result_pool = ctx.enter_context(tc.tile_pool(name="result", bufs=8))
-        dg_psum = ctx.enter_context(tc.psum_pool(name="dg_psum", bufs=3))
-        product_psum = ctx.enter_context(tc.psum_pool(name="product_psum", bufs=2))
-
-        def bank_copy(index):
-            return nc.vector.tensor_copy if index % 2 == 0 else nc.scalar.copy
+        result_pool = ctx.enter_context(tc.tile_pool(name="result", bufs=3 * TILES))
+        banks = ctx.enter_context(tc.psum_pool(name="banks", bufs=PSUM_BANKS))
 
         ident = keep.tile([P, P], F32)
         make_identity(nc, ident[:])
+        ident_bf16 = keep.tile([P, P], BF16)
+        make_identity(nc, ident_bf16[:])
 
-        k3_raw = []
-        for j in range(GROUPS):
+        def load_rows(rows):
             raw = raw_pool.tile([P, WINDOW], BF16)
-            nc.sync.dma_start(out=raw[:], in_=k3_rows[:, j, :])
-            k3_raw.append(raw)
+            nc.sync.dma_start(out=raw[:], in_=rows)
+            return raw
+
+        dy_raw = [load_rows(dy_rows[:, s, :]) for s in range(TILES)]
         k2_rows = keep.tile([P, GROUPS, R], BF16)
-        dy_raw = []
-        for s in range(ROWS_PER_PARTITION):
-            raw = raw_pool.tile([P, WINDOW], BF16)
-            nc.sync.dma_start(out=raw[:], in_=dy_rows[:, s, :])
-            dy_raw.append(raw)
-            if s == TILES - 1:
-                nc.sync.dma_start(out=k2_rows[:], in_=k2.rearrange("j i o -> i j o"))
-
-        k3_codes = keep.tile([P, PASSES, COEFFS], U32, align_bytes=64)
-        k3_scales = keep.tile([P, PASSES, COEFFS], U8, align_bytes=64)
-        for j in range(GROUPS):
-            cols = slice(j * R, (j + 1) * R)
-            quantise_row_tile(
-                nc, pools, bank_copy(j), ident, k3_raw[j], E4M3X4, k3_codes[:, :, cols], k3_scales[:, :, cols]
-            )
+        nc.sync.dma_start(out=k2_rows[:], in_=k2.rearrange("j i o -> i j o"))
+        k3_raw = [load_rows(k3_rows[:, j, :]) for j in range(GROUPS)]
+        dy_raw.extend([load_rows(dy_rows[:, s, :]) for s in range(TILES, ROWS_PER_PARTITION)])
 
         def quantise_block(b):
             dy_codes = operand_pool.tile([P, PASSES, BLOCK], U32, align_bytes=64)
@@ -101,7 +86,7 @@ def tile_switchnet_fstar_pb_t_kernel(tc, h_switch, k2, b2, k3, b3, grad_out, out
             for t in range(TILES):
                 cols = slice(t * P, (t + 1) * P)
                 quantise_row_tile(
-                    nc, pools, bank_copy(t), ident, dy_raw[b * TILES + t], E5M2X4,
+                    nc, banks, grouped_pool, ident, dy_raw[b * TILES + t], E5M2X4,
                     dy_codes[:, :, cols], dy_scales[:, :, cols],
                 )
             return dy_codes, dy_scales
@@ -110,7 +95,7 @@ def tile_switchnet_fstar_pb_t_kernel(tc, h_switch, k2, b2, k3, b3, grad_out, out
             dgT = dg_pool.tile([P, GROUPS, BLOCK], F32)
             for j in range(GROUPS):
                 cols = slice(j * R, (j + 1) * R)
-                acc = dg_psum.tile([P, BLOCK], F32)
+                acc = banks.tile([P, BLOCK], F32, tag="bank")
                 for g in range(PASSES):
                     nc.tensor.matmul_mx(
                         out=acc[:],
@@ -121,12 +106,12 @@ def tile_switchnet_fstar_pb_t_kernel(tc, h_switch, k2, b2, k3, b3, grad_out, out
                         start=(g == 0),
                         stop=(g == PASSES - 1),
                     )
-                bank_copy(j)(out=dgT[:, j, :], in_=acc[:])
+                nc.vector.tensor_copy(out=dgT[:, j, :], in_=acc[:])
             return dgT
 
         def second_matmul(b, dgT):
             for t in range(TILES):
-                product = product_psum.tile([P, COEFFS], F32)
+                product = banks.tile([P, COEFFS], F32, tag="bank")
                 for j in range(GROUPS):
                     nc.tensor.matmul(
                         out=product[:, j * R : (j + 1) * R],
@@ -141,13 +126,19 @@ def tile_switchnet_fstar_pb_t_kernel(tc, h_switch, k2, b2, k3, b3, grad_out, out
 
         operands = quantise_block(0)
 
-        k2_f32 = keep.tile([P, GROUPS, R], F32)
-        nc.vector.tensor_copy(out=k2_f32[:], in_=k2_rows[:])
-        k2T_psum = pools["flipped"].tile([P, GROUPS, R], F32, tag="flipped")
+        k2T_psum = banks.tile([P, GROUPS, R], BF16, tag="bank")
         for j in range(GROUPS):
-            nc.tensor.transpose(k2T_psum[:, j, :], k2_f32[:, j, :], ident[:])
+            nc.tensor.transpose(k2T_psum[:, j, :], k2_rows[:, j, :], ident_bf16[:])
         k2T = keep.tile([P, GROUPS, R], F32)
         nc.vector.tensor_copy(out=k2T[:], in_=k2T_psum[:])
+
+        k3_codes = keep.tile([P, PASSES, COEFFS], U32, align_bytes=64)
+        k3_scales = keep.tile([P, PASSES, COEFFS], U8, align_bytes=64)
+        for j in range(GROUPS):
+            cols = slice(j * R, (j + 1) * R)
+            quantise_row_tile(
+                nc, banks, grouped_pool, ident, k3_raw[j], E4M3X4, k3_codes[:, :, cols], k3_scales[:, :, cols]
+            )
 
         for b in range(BLOCKS):
             dgT = mx_matmul(*operands)

@@ -25,6 +25,7 @@ TILES = BLOCK // P
 BLOCKS = SAMPLES // BLOCK
 ROWS_PER_PARTITION = SAMPLES // P
 PSUM_BANKS = 8
+LEAD = TILES + 1
 
 FLOPS = 2 * SAMPLES * COEFFS * WINDOW + 2 * SAMPLES * COEFFS * R
 BYTES = 2 * SAMPLES * WINDOW + 2 * COEFFS * WINDOW + 2 * GROUPS * R * R + 4 * SAMPLES * COEFFS
@@ -59,7 +60,7 @@ def tile_switchnet_fstar_pb_t_kernel(tc, h_switch, k2, b2, k3, b3, grad_out, out
         keep = ctx.enter_context(tc.tile_pool(name="keep", bufs=1))
         raw_pool = ctx.enter_context(tc.tile_pool(name="raw", bufs=GROUPS + BLOCKS * TILES))
         grouped_pool = ctx.enter_context(tc.tile_pool(name="grouped", bufs=4))
-        operand_pool = ctx.enter_context(tc.tile_pool(name="operand", bufs=2))
+        operand_pool = ctx.enter_context(tc.tile_pool(name="operand", bufs=3))
         dg_pool = ctx.enter_context(tc.tile_pool(name="dg", bufs=2))
         result_pool = ctx.enter_context(tc.tile_pool(name="result", bufs=3 * TILES))
         banks = ctx.enter_context(tc.psum_pool(name="banks", bufs=PSUM_BANKS))
@@ -80,16 +81,19 @@ def tile_switchnet_fstar_pb_t_kernel(tc, h_switch, k2, b2, k3, b3, grad_out, out
         k3_raw = [load_rows(k3_rows[:, j, :]) for j in range(GROUPS)]
         dy_raw.extend([load_rows(dy_rows[:, s, :]) for s in range(TILES, ROWS_PER_PARTITION)])
 
-        def quantise_block(b):
-            dy_codes = operand_pool.tile([P, PASSES, BLOCK], U32, align_bytes=64)
-            dy_scales = operand_pool.tile([P, PASSES, BLOCK], U8, align_bytes=64)
-            for t in range(TILES):
-                cols = slice(t * P, (t + 1) * P)
-                quantise_row_tile(
-                    nc, banks, grouped_pool, ident, dy_raw[b * TILES + t], E5M2X4,
-                    dy_codes[:, :, cols], dy_scales[:, :, cols],
-                )
-            return dy_codes, dy_scales
+        operands = []
+
+        def quantise_dy_tile(n):
+            t = n % TILES
+            if t == 0:
+                dy_codes = operand_pool.tile([P, PASSES, BLOCK], U32, align_bytes=64)
+                dy_scales = operand_pool.tile([P, PASSES, BLOCK], U8, align_bytes=64)
+                operands.append((dy_codes, dy_scales))
+            codes, scales = operands[n // TILES]
+            cols = slice(t * P, (t + 1) * P)
+            quantise_row_tile(
+                nc, banks, grouped_pool, ident, dy_raw[n], E5M2X4, codes[:, :, cols], scales[:, :, cols]
+            )
 
         def mx_matmul(dy_codes, dy_scales):
             dgT = dg_pool.tile([P, GROUPS, BLOCK], F32)
@@ -109,22 +113,23 @@ def tile_switchnet_fstar_pb_t_kernel(tc, h_switch, k2, b2, k3, b3, grad_out, out
                 nc.vector.tensor_copy(out=dgT[:, j, :], in_=acc[:])
             return dgT
 
-        def second_matmul(b, dgT):
-            for t in range(TILES):
-                product = banks.tile([P, COEFFS], F32, tag="bank")
-                for j in range(GROUPS):
-                    nc.tensor.matmul(
-                        out=product[:, j * R : (j + 1) * R],
-                        lhsT=dgT[:, j, t * P : (t + 1) * P],
-                        rhs=k2T[:, j, :],
-                        start=True,
-                        stop=True,
-                    )
-                result = result_pool.tile([P, COEFFS], F32)
-                nc.scalar.copy(out=result[:], in_=product[:])
-                nc.sync.dma_start(out=out_rows[:, b * TILES + t, :], in_=result[:])
+        def second_matmul(n, dgT):
+            t = n % TILES
+            product = banks.tile([P, COEFFS], F32, tag="bank")
+            for j in range(GROUPS):
+                nc.tensor.matmul(
+                    out=product[:, j * R : (j + 1) * R],
+                    lhsT=dgT[:, j, t * P : (t + 1) * P],
+                    rhs=k2T[:, j, :],
+                    start=True,
+                    stop=True,
+                )
+            result = result_pool.tile([P, COEFFS], F32)
+            nc.scalar.copy(out=result[:], in_=product[:])
+            nc.sync.dma_start(out=out_rows[:, n, :], in_=result[:])
 
-        operands = quantise_block(0)
+        for n in range(TILES):
+            quantise_dy_tile(n)
 
         k2T_psum = banks.tile([P, GROUPS, R], BF16, tag="bank")
         for j in range(GROUPS):
@@ -140,8 +145,12 @@ def tile_switchnet_fstar_pb_t_kernel(tc, h_switch, k2, b2, k3, b3, grad_out, out
                 nc, banks, grouped_pool, ident, k3_raw[j], E4M3X4, k3_codes[:, :, cols], k3_scales[:, :, cols]
             )
 
+        for n in range(TILES, LEAD):
+            quantise_dy_tile(n)
+
         for b in range(BLOCKS):
-            dgT = mx_matmul(*operands)
-            if b + 1 < BLOCKS:
-                operands = quantise_block(b + 1)
-            second_matmul(b, dgT)
+            dgT = mx_matmul(*operands[b])
+            for n in range(b * TILES, (b + 1) * TILES):
+                if n + LEAD < ROWS_PER_PARTITION:
+                    quantise_dy_tile(n + LEAD)
+                second_matmul(n, dgT)

@@ -25,13 +25,13 @@ TILES = BLOCK // P
 BLOCKS = SAMPLES // BLOCK
 ROWS_PER_PARTITION = SAMPLES // P
 PSUM_BANKS = 8
-LEAD = TILES + 1
+LEAD = TILES + 2
 
 FLOPS = 2 * SAMPLES * COEFFS * WINDOW + 2 * SAMPLES * COEFFS * R
 BYTES = 2 * SAMPLES * WINDOW + 2 * COEFFS * WINDOW + 2 * GROUPS * R * R + 4 * SAMPLES * COEFFS
 
 
-def quantise_row_tile(nc, banks, grouped_pool, ident, raw, fp8x4, codes, scales):
+def pack_row_tile(nc, banks, grouped_pool, ident, raw, copy):
     words = raw[:].bitcast(F32)
     flipped = banks.tile([P, PASSES, HALVES, P], F32, tag="bank")
     for g in range(PASSES):
@@ -39,7 +39,11 @@ def quantise_row_tile(nc, banks, grouped_pool, ident, raw, fp8x4, codes, scales)
             first = (g * HALVES + u) * P
             nc.tensor.transpose(flipped[:, g, u, :], words[:, first : first + P], ident[:])
     grouped = grouped_pool.tile([P, PASSES, P, HALVES], F32, align_bytes=64)
-    nc.scalar.copy(out=grouped[:], in_=flipped[:].rearrange("p g u r -> p g r u"))
+    copy(out=grouped[:], in_=flipped[:].rearrange("p g u r -> p g r u"))
+    return grouped
+
+
+def quantise_row_tile(nc, grouped, fp8x4, codes, scales):
     for g in range(PASSES):
         nc.vector.quantize_mx(
             out=codes[:, g, :].bitcast(fp8x4),
@@ -76,44 +80,52 @@ def tile_switchnet_fstar_pb_t_kernel(tc, h_switch, k2, b2, k3, b3, grad_out, out
             return raw
 
         dy_raw = [load_rows(dy_rows[:, s, :]) for s in range(TILES)]
+        k3_raw = [load_rows(k3_rows[:, j, :]) for j in range(GROUPS)]
         k2_rows = keep.tile([P, GROUPS, R], BF16)
         nc.sync.dma_start(out=k2_rows[:], in_=k2.rearrange("j i o -> i j o"))
-        k3_raw = [load_rows(k3_rows[:, j, :]) for j in range(GROUPS)]
         dy_raw.extend([load_rows(dy_rows[:, s, :]) for s in range(TILES, ROWS_PER_PARTITION)])
 
-        operands = []
+        k3_codes = keep.tile([P, PASSES, COEFFS], U32, align_bytes=64)
+        k3_scales = keep.tile([P, PASSES, COEFFS], U8, align_bytes=64)
+        operands = {}
+        grouped_tiles = {}
 
-        def quantise_dy_tile(n):
-            t = n % TILES
-            if t == 0:
+        def pack_dy(n):
+            copy = nc.vector.tensor_copy if n == 1 else nc.scalar.copy
+            grouped_tiles[n] = pack_row_tile(nc, banks, grouped_pool, ident, dy_raw[n], copy)
+
+        def quantise_dy(n):
+            if n % TILES == 0:
                 dy_codes = operand_pool.tile([P, PASSES, BLOCK], U32, align_bytes=64)
                 dy_scales = operand_pool.tile([P, PASSES, BLOCK], U8, align_bytes=64)
-                operands.append((dy_codes, dy_scales))
+                operands[n // TILES] = (dy_codes, dy_scales)
             codes, scales = operands[n // TILES]
-            cols = slice(t * P, (t + 1) * P)
-            quantise_row_tile(
-                nc, banks, grouped_pool, ident, dy_raw[n], E5M2X4, codes[:, :, cols], scales[:, :, cols]
-            )
+            cols = slice(n % TILES * P, (n % TILES + 1) * P)
+            quantise_row_tile(nc, grouped_tiles[n], E5M2X4, codes[:, :, cols], scales[:, :, cols])
 
-        def mx_matmul(dy_codes, dy_scales):
-            dgT = dg_pool.tile([P, GROUPS, BLOCK], F32)
-            for j in range(GROUPS):
-                cols = slice(j * R, (j + 1) * R)
-                acc = banks.tile([P, BLOCK], F32, tag="bank")
-                for g in range(PASSES):
-                    nc.tensor.matmul_mx(
-                        out=acc[:],
-                        lhsT=k3_codes[:, g, cols].bitcast(E4M3X4),
-                        lhsT_scale=k3_scales[:, g, cols],
-                        rhs=dy_codes[:, g, :].bitcast(E5M2X4),
-                        rhs_scale=dy_scales[:, g, :],
-                        start=(g == 0),
-                        stop=(g == PASSES - 1),
-                    )
-                nc.vector.tensor_copy(out=dgT[:, j, :], in_=acc[:])
-            return dgT
+        dgTs = {}
 
-        def second_matmul(n, dgT):
+        def mx_group(b, j, copy):
+            if j == 0:
+                dgT = dg_pool.tile([P, GROUPS, BLOCK], F32)
+                dgTs[b] = dgT
+            dy_codes, dy_scales = operands[b]
+            cols = slice(j * R, (j + 1) * R)
+            acc = banks.tile([P, BLOCK], F32, tag="bank")
+            for g in range(PASSES):
+                nc.tensor.matmul_mx(
+                    out=acc[:],
+                    lhsT=k3_codes[:, g, cols].bitcast(E4M3X4),
+                    lhsT_scale=k3_scales[:, g, cols],
+                    rhs=dy_codes[:, g, :].bitcast(E5M2X4),
+                    rhs_scale=dy_scales[:, g, :],
+                    start=(g == 0),
+                    stop=(g == PASSES - 1),
+                )
+            copy(out=dgTs[b][:, j, :], in_=acc[:])
+
+        def second_matmul(n):
+            dgT = dgTs[n // TILES]
             t = n % TILES
             product = banks.tile([P, COEFFS], F32, tag="bank")
             for j in range(GROUPS):
@@ -128,29 +140,43 @@ def tile_switchnet_fstar_pb_t_kernel(tc, h_switch, k2, b2, k3, b3, grad_out, out
             nc.scalar.copy(out=result[:], in_=product[:])
             nc.sync.dma_start(out=out_rows[:, n, :], in_=result[:])
 
-        for n in range(TILES):
-            quantise_dy_tile(n)
+        def k2_transposes():
+            k2T_psum = banks.tile([P, GROUPS, R], BF16, tag="bank")
+            for j in range(GROUPS):
+                nc.tensor.transpose(k2T_psum[:, j, :], k2_rows[:, j, :], ident_bf16[:])
+            return k2T_psum
 
-        k2T_psum = banks.tile([P, GROUPS, R], BF16, tag="bank")
-        for j in range(GROUPS):
-            nc.tensor.transpose(k2T_psum[:, j, :], k2_rows[:, j, :], ident_bf16[:])
         k2T = keep.tile([P, GROUPS, R], F32)
-        nc.vector.tensor_copy(out=k2T[:], in_=k2T_psum[:])
+        head = [("dy", n) for n in range(TILES)] + [("k3", j) for j in range(GROUPS)]
+        k3_grouped = {}
+        for step in range(len(head) + 3):
+            if step < len(head):
+                kind, n = head[step]
+                if kind == "dy":
+                    pack_dy(n)
+                else:
+                    k3_grouped[n] = pack_row_tile(nc, banks, grouped_pool, ident, k3_raw[n], nc.scalar.copy)
+            if 1 <= step <= len(head):
+                kind, n = head[step - 1]
+                if kind == "dy":
+                    quantise_dy(n)
+                else:
+                    cols = slice(n * R, (n + 1) * R)
+                    quantise_row_tile(nc, k3_grouped[n], E4M3X4, k3_codes[:, :, cols], k3_scales[:, :, cols])
+            if step == len(head):
+                nc.vector.tensor_copy(out=k2T[:], in_=k2_transposes()[:])
+            if step >= TILES + 3:
+                j = step - TILES - 3
+                mx_group(0, j, nc.vector.tensor_copy if j == GROUPS - 1 else nc.scalar.copy)
 
-        k3_codes = keep.tile([P, PASSES, COEFFS], U32, align_bytes=64)
-        k3_scales = keep.tile([P, PASSES, COEFFS], U8, align_bytes=64)
-        for j in range(GROUPS):
-            cols = slice(j * R, (j + 1) * R)
-            quantise_row_tile(
-                nc, banks, grouped_pool, ident, k3_raw[j], E4M3X4, k3_codes[:, :, cols], k3_scales[:, :, cols]
-            )
-
-        for n in range(TILES, LEAD):
-            quantise_dy_tile(n)
-
-        for b in range(BLOCKS):
-            dgT = mx_matmul(*operands[b])
-            for n in range(b * TILES, (b + 1) * TILES):
-                if n + LEAD < ROWS_PER_PARTITION:
-                    quantise_dy_tile(n + LEAD)
-                second_matmul(n, dgT)
+        prepared = TILES
+        for n in range(ROWS_PER_PARTITION):
+            target = min(prepared + 2, n + LEAD + 1, ROWS_PER_PARTITION)
+            for m in range(prepared, target):
+                pack_dy(m)
+                quantise_dy(m)
+            prepared = target
+            if n % TILES == TILES - 1 and n // TILES + 1 < BLOCKS:
+                for j in range(GROUPS):
+                    mx_group(n // TILES + 1, j, nc.vector.tensor_copy)
+            second_matmul(n)

@@ -140,6 +140,26 @@ def tile_switchnet_fstar_pb_t_kernel(tc, h_switch, k2, b2, k3, b3, grad_out, out
             nc.scalar.copy(out=result[:], in_=product[:])
             nc.sync.dma_start(out=out_rows[:, n, :], in_=result[:])
 
+        def last_second_matmul(n):
+            dgT = dgTs[n // TILES]
+            t = n % TILES
+            for half, copy, queue in ((0, nc.vector.tensor_copy, nc.sync), (1, nc.scalar.copy, nc.scalar)):
+                product = banks.tile([P, COEFFS // 2], F32, tag="bank")
+                for i in range(GROUPS // 2):
+                    j = half * GROUPS // 2 + i
+                    nc.tensor.matmul(
+                        out=product[:, i * R : (i + 1) * R],
+                        lhsT=dgT[:, j, t * P : (t + 1) * P],
+                        rhs=k2T[:, j, :],
+                        start=True,
+                        stop=True,
+                    )
+                result = result_pool.tile([P, COEFFS // 2], F32)
+                copy(out=result[:], in_=product[:])
+                queue.dma_start(
+                    out=out_rows[:, n, half * COEFFS // 2 : (half + 1) * COEFFS // 2], in_=result[:]
+                )
+
         def k2_transposes():
             k2T_psum = banks.tile([P, GROUPS, R], BF16, tag="bank")
             for j in range(GROUPS):
@@ -147,6 +167,16 @@ def tile_switchnet_fstar_pb_t_kernel(tc, h_switch, k2, b2, k3, b3, grad_out, out
             return k2T_psum
 
         k2T = keep.tile([P, GROUPS, R], F32)
+        zeros = keep.tile([P, BLOCK], BF16)
+        nc.vector.memset(zeros[:], 0.0)
+        idle_bank = banks.tile([P, BLOCK], F32, tag="bank")
+
+        def warm_up():
+            nc.tensor.matmul(out=idle_bank[:], lhsT=zeros[:, :P], rhs=zeros[:], start=True, stop=True)
+
+        for again in range(4):
+            warm_up()
+
         head = [("dy", n) for n in range(TILES)] + [("k3", j) for j in range(GROUPS)]
         k3_grouped = {}
         for step in range(len(head) + 3):
@@ -156,6 +186,8 @@ def tile_switchnet_fstar_pb_t_kernel(tc, h_switch, k2, b2, k3, b3, grad_out, out
                     pack_dy(n)
                 else:
                     k3_grouped[n] = pack_row_tile(nc, banks, grouped_pool, ident, k3_raw[n], nc.scalar.copy)
+            if 1 <= step <= 5:
+                warm_up()
             if 1 <= step <= len(head):
                 kind, n = head[step - 1]
                 if kind == "dy":
@@ -179,4 +211,7 @@ def tile_switchnet_fstar_pb_t_kernel(tc, h_switch, k2, b2, k3, b3, grad_out, out
             if n % TILES == TILES - 1 and n // TILES + 1 < BLOCKS:
                 for j in range(GROUPS):
                     mx_group(n // TILES + 1, j, nc.vector.tensor_copy)
-            second_matmul(n)
+            if n < ROWS_PER_PARTITION - 1:
+                second_matmul(n)
+            else:
+                last_second_matmul(n)

@@ -203,7 +203,8 @@ def tile_switchnet_fstar_pb_t_kernel(tc, h_switch, k2, b2, k3, b3, grad_out, out
 
         prepared = TILES
         for n in range(ROWS_PER_PARTITION):
-            target = min(prepared + 2, n + LEAD + 1, ROWS_PER_PARTITION)
+            ahead = n + LEAD + (2 if n % TILES == TILES - 2 else 1)
+            target = min(prepared + 2, ahead, ROWS_PER_PARTITION)
             for m in range(prepared, target):
                 pack_dy(m)
                 quantise_dy(m)

from contextlib import ExitStack

import concourse.mybir as mybir
from concourse.masks import make_identity

F32 = mybir.dt.float32
BF16 = mybir.dt.bfloat16
U32 = mybir.dt.uint32
U8 = mybir.dt.uint8
E4M3X4 = mybir.dt.float8_e4m3fn_x4
E5M2X4 = mybir.dt.float8_e5m2_x4

P = 128
SAMPLES = 4096
WINDOW = 1024
GROUPS = 4
R = 128
COEFFS = GROUPS * R

K_PASS = 4 * P
PASSES = WINDOW // K_PASS
HALVES = 2
BLOCK = 512
TILES = BLOCK // P
BLOCKS = SAMPLES // BLOCK
ROWS_PER_PARTITION = SAMPLES // P
PSUM_BANKS = 8
LEAD = TILES + 2

FLOPS = 2 * SAMPLES * COEFFS * WINDOW + 2 * SAMPLES * COEFFS * R
BYTES = 2 * SAMPLES * WINDOW + 2 * COEFFS * WINDOW + 2 * GROUPS * R * R + 4 * SAMPLES * COEFFS


def pack_row_tile(nc, banks, grouped_pool, ident, raw, copy):
    words = raw[:].bitcast(F32)
    flipped = banks.tile([P, PASSES, HALVES, P], F32, tag="bank")
    for g in range(PASSES):
        for u in range(HALVES):
            first = (g * HALVES + u) * P
            nc.tensor.transpose(flipped[:, g, u, :], words[:, first : first + P], ident[:])
    grouped = grouped_pool.tile([P, PASSES, P, HALVES], F32, align_bytes=64)
    copy(out=grouped[:], in_=flipped[:].rearrange("p g u r -> p g r u"))
    return grouped


def quantise_row_tile(nc, grouped, fp8x4, codes, scales):
    for g in range(PASSES):
        nc.vector.quantize_mx(
            out=codes[:, g, :].bitcast(fp8x4),
            scales=scales[:, g, :],
            in_=grouped[:, g, :, :].rearrange("p r u -> p (r u)").bitcast(BF16),
        )


def tile_switchnet_fstar_pb_t_kernel(tc, h_switch, k2, b2, k3, b3, grad_out, out):
    nc = tc.nc

    dy_rows = grad_out.rearrange("(p s) x y c -> p s (x y c)", s=ROWS_PER_PARTITION)
    out_rows = out.rearrange("(p s) j i -> p s (j i)", s=ROWS_PER_PARTITION)
    k3_rows = k3[0, :, :].rearrange("(j p) k -> p j k", p=P)

    with ExitStack() as ctx:
        ctx.enter_context(tc.manual_schedule())
        keep = ctx.enter_context(tc.tile_pool(name="keep", bufs=1))
        raw_pool = ctx.enter_context(tc.tile_pool(name="raw", bufs=GROUPS + BLOCKS * TILES))
        grouped_pool = ctx.enter_context(tc.tile_pool(name="grouped", bufs=4))
        operand_pool = ctx.enter_context(tc.tile_pool(name="operand", bufs=3))
        dg_pool = ctx.enter_context(tc.tile_pool(name="dg", bufs=2))
        result_pool = ctx.enter_context(tc.tile_pool(name="result", bufs=3 * TILES))
        banks = ctx.enter_context(tc.psum_pool(name="banks", bufs=PSUM_BANKS))

        ident = keep.tile([P, P], F32)
        make_identity(nc, ident[:])
        ident_bf16 = keep.tile([P, P], BF16)
        make_identity(nc, ident_bf16[:])

        def load_rows(rows):
            raw = raw_pool.tile([P, WINDOW], BF16)
            nc.sync.dma_start(out=raw[:], in_=rows)
            return raw

        dy_raw = [load_rows(dy_rows[:, s, :]) for s in range(TILES)]
        k3_raw = [load_rows(k3_rows[:, j, :]) for j in range(GROUPS)]
        k2_rows = keep.tile([P, GROUPS, R], BF16)
        nc.sync.dma_start(out=k2_rows[:], in_=k2.rearrange("j i o -> i j o"))
        dy_raw.extend([load_rows(dy_rows[:, s, :]) for s in range(TILES, ROWS_PER_PARTITION)])

        k3_codes = keep.tile([P, PASSES, COEFFS], U32, align_bytes=64)
        k3_scales = keep.tile([P, PASSES, COEFFS], U8, align_bytes=64)
        operands = {}
        grouped_tiles = {}

        def pack_dy(n):
            copy = nc.vector.tensor_copy if n == 1 else nc.scalar.copy
            grouped_tiles[n] = pack_row_tile(nc, banks, grouped_pool, ident, dy_raw[n], copy)

        def quantise_dy(n):
            if n % TILES == 0:
                dy_codes = operand_pool.tile([P, PASSES, BLOCK], U32, align_bytes=64)
                dy_scales = operand_pool.tile([P, PASSES, BLOCK], U8, align_bytes=64)
                operands[n // TILES] = (dy_codes, dy_scales)
            codes, scales = operands[n // TILES]
            cols = slice(n % TILES * P, (n % TILES + 1) * P)
            quantise_row_tile(nc, grouped_tiles[n], E5M2X4, codes[:, :, cols], scales[:, :, cols])

        dgTs = {}

        def mx_group(b, j, copy):
            if j == 0:
                dgT = dg_pool.tile([P, GROUPS, BLOCK], F32)
                dgTs[b] = dgT
            dy_codes, dy_scales = operands[b]
            cols = slice(j * R, (j + 1) * R)
            acc = banks.tile([P, BLOCK], F32, tag="bank")
            for g in range(PASSES):
                nc.tensor.matmul_mx(
                    out=acc[:],
                    lhsT=k3_codes[:, g, cols].bitcast(E4M3X4),
                    lhsT_scale=k3_scales[:, g, cols],
                    rhs=dy_codes[:, g, :].bitcast(E5M2X4),
                    rhs_scale=dy_scales[:, g, :],
                    start=(g == 0),
                    stop=(g == PASSES - 1),
                )
            copy(out=dgTs[b][:, j, :], in_=acc[:])

        def second_matmul(n):
            dgT = dgTs[n // TILES]
            t = n % TILES
            product = banks.tile([P, COEFFS], F32, tag="bank")
            for j in range(GROUPS):
                nc.tensor.matmul(
                    out=product[:, j * R : (j + 1) * R],
                    lhsT=dgT[:, j, t * P : (t + 1) * P],
                    rhs=k2T[:, j, :],
                    start=True,
                    stop=True,
                )
            result = result_pool.tile([P, COEFFS], F32)
            nc.scalar.copy(out=result[:], in_=product[:])
            nc.sync.dma_start(out=out_rows[:, n, :], in_=result[:])

        def last_second_matmul(n):
            dgT = dgTs[n // TILES]
            t = n % TILES
            for half, copy, queue in ((0, nc.vector.tensor_copy, nc.sync), (1, nc.scalar.copy, nc.scalar)):
                product = banks.tile([P, COEFFS // 2], F32, tag="bank")
                for i in range(GROUPS // 2):
                    j = half * GROUPS // 2 + i
                    nc.tensor.matmul(
                        out=product[:, i * R : (i + 1) * R],
                        lhsT=dgT[:, j, t * P : (t + 1) * P],
                        rhs=k2T[:, j, :],
                        start=True,
                        stop=True,
                    )
                result = result_pool.tile([P, COEFFS // 2], F32)
                copy(out=result[:], in_=product[:])
                queue.dma_start(
                    out=out_rows[:, n, half * COEFFS // 2 : (half + 1) * COEFFS // 2], in_=result[:]
                )

        def k2_transposes():
            k2T_psum = banks.tile([P, GROUPS, R], BF16, tag="bank")
            for j in range(GROUPS):
                nc.tensor.transpose(k2T_psum[:, j, :], k2_rows[:, j, :], ident_bf16[:])
            return k2T_psum

        k2T = keep.tile([P, GROUPS, R], F32)
        zeros = keep.tile([P, BLOCK], BF16)
        nc.vector.memset(zeros[:], 0.0)
        idle_bank = banks.tile([P, BLOCK], F32, tag="bank")

        def warm_up():
            nc.tensor.matmul(out=idle_bank[:], lhsT=zeros[:, :P], rhs=zeros[:], start=True, stop=True)

        for again in range(4):
            warm_up()

        head = [("dy", n) for n in range(TILES)] + [("k3", j) for j in range(GROUPS)]
        k3_grouped = {}
        for step in range(len(head) + 3):
            if step < len(head):
                kind, n = head[step]
                if kind == "dy":
                    pack_dy(n)
                else:
                    k3_grouped[n] = pack_row_tile(nc, banks, grouped_pool, ident, k3_raw[n], nc.scalar.copy)
            if 1 <= step <= 5:
                warm_up()
            if 1 <= step <= len(head):
                kind, n = head[step - 1]
                if kind == "dy":
                    quantise_dy(n)
                else:
                    cols = slice(n * R, (n + 1) * R)
                    quantise_row_tile(nc, k3_grouped[n], E4M3X4, k3_codes[:, :, cols], k3_scales[:, :, cols])
            if step == len(head):
                nc.vector.tensor_copy(out=k2T[:], in_=k2_transposes()[:])
            if step >= TILES + 3:
                j = step - TILES - 3
                mx_group(0, j, nc.vector.tensor_copy if j == GROUPS - 1 else nc.scalar.copy)

        prepared = TILES
        for n in range(ROWS_PER_PARTITION):
            ahead = n + LEAD + (2 if n % TILES == TILES - 2 else 1)
            target = min(prepared + 2, ahead, ROWS_PER_PARTITION)
            for m in range(prepared, target):
                pack_dy(m)
                quantise_dy(m)
            prepared = target
            if n % TILES == TILES - 1 and n // TILES + 1 < BLOCKS:
                for j in range(GROUPS):
                    mx_group(n // TILES + 1, j, nc.vector.tensor_copy)
            if n < ROWS_PER_PARTITION - 1:
                second_matmul(n)
            else:
                last_second_matmul(n)
